import numpy as np
import ml_dtypes


def mxq(x, axis, fmt="e4m3"):
    dtype, down = {"e4m3": (ml_dtypes.float8_e4m3fn, 7), "e5m2": (ml_dtypes.float8_e5m2, 14)}[fmt]
    v = np.moveaxis(np.asarray(x, np.float32).astype(ml_dtypes.bfloat16).astype(np.float64), axis, -1)
    blocks = v.reshape(v.shape[:-1] + (-1, 32))
    amax = np.abs(blocks).max(-1, keepdims=True)
    byte = np.maximum(np.where(amax > 0, np.frexp(amax)[1] - 1 + 127, 0) - down, 1)
    scale = np.exp2(byte - 127.0)
    codes = (blocks / scale).astype(np.float32).astype(dtype).astype(np.float64)
    return np.moveaxis((codes * scale).reshape(v.shape), -1, axis)


WIDE = False


def mx_kscale(k):
    if not WIDE:
        return np.ones(k)
    levels = np.array([10, -10, 5, -5, 0])
    a = np.random.permutation(np.resize(levels, k // 512 * 4)).reshape(k // 512, 4)
    idx = np.arange(k)
    return np.exp2(a[idx // 512, idx % 128 // 32])


BF16 = ml_dtypes.bfloat16


def bf(x):
    return np.asarray(x, np.float32).astype(BF16)


def f64(x):
    return np.asarray(x).astype(np.float64)


B, C, D = 1024, 2048, 1024


def setup_inputs():
    u = np.exp2(np.round(np.log2(mx_kscale(D)) / 2))
    a = 1.0 / np.sqrt(D)
    x = (np.random.standard_normal((B, D)) + np.random.uniform(-1.0, 1.0, (B, 1))) * a
    mean = np.random.uniform(0.0, 1.0, (C, D)) * np.random.uniform(0.5, 1.5, (C, 1)) * a
    sigma = np.log1p(np.exp(np.random.uniform(0.0, 1.0, (C, D)))) * u
    rho = np.log(np.expm1(sigma))
    return {"x": bf(x * u), "mean": bf(mean * u), "rho": bf(rho)}


def reference(x, mean, rho):
    x, mean, rho = f64(x), f64(mean), f64(rho)
    sigma = np.log1p(np.exp(rho))
    w = 1.0 / (2.0 * sigma * sigma)
    quad = (
        (mxq(x * x, 1, "e4m3") @ mxq(w, 1, "e4m3").T)
        - 2.0 * (mxq(x, 1, "e4m3") @ mxq(mean * w, 1, "e4m3").T)
        + np.sum(mean * mean * w, axis=-1)
    )
    return np.exp(-quad)

@@ -1,0 +1,328 @@
+from contextlib import ExitStack
+
+import concourse.mybir as mybir
+from concourse.masks import make_identity
+
+FLOPS = 2 * 2 * 1024 * 2048 * 1024
+
+P = 128
+NB = 8
+NCH = 4
+F32 = mybir.dt.float32
+BF16 = mybir.dt.bfloat16
+U32 = mybir.dt.uint32
+U8 = mybir.dt.uint8
+FP8X4 = mybir.dt.float8_e4m3fn_x4
+ACT = mybir.ActivationFunctionType
+ALU = mybir.AluOpType
+
+
+def tile_dynamic_estimator_kernel(tc, x, mean, rho, out):
+    nc = tc.nc
+    with ExitStack() as ctx:
+        consts = ctx.enter_context(tc.tile_pool(name="consts", bufs=1))
+        xraw_pool = ctx.enter_context(tc.tile_pool(name="xraw", bufs=4))
+        xstage = ctx.enter_context(tc.tile_pool(name="xstage", bufs=2))
+        xkeep = ctx.enter_context(tc.tile_pool(name="xkeep", bufs=1))
+        raw_pool = ctx.enter_context(tc.tile_pool(name="raw", bufs=2))
+        chain_pool = ctx.enter_context(tc.tile_pool(name="chain", bufs=2))
+        work = ctx.enter_context(tc.tile_pool(name="work", bufs=1))
+        codes = ctx.enter_context(tc.tile_pool(name="codes", bufs=2))
+        pre_pool = ctx.enter_context(tc.tile_pool(name="pre", bufs=3))
+        ps_tr = ctx.enter_context(tc.psum_pool(name="ps_tr", bufs=2))
+        ps_mt = ctx.enter_context(tc.psum_pool(name="ps_mt", bufs=2))
+        ps_s = ctx.enter_context(tc.psum_pool(name="ps_s", bufs=2))
+        ps_mx = ctx.enter_context(tc.psum_pool(name="ps_mx", bufs=2))
+
+        rho_raw = {}
+        mean_raw = {}
+        x_raw = {}
+        chain = {}
+        tprod = {}
+        vprod = {}
+        wg = {}
+        mwg = {}
+        cw = {}
+        sb = {}
+        pre = {}
+        rts = {}
+        mts = {}
+
+        def load_cls(store, src, i, split):
+            raw_t = raw_pool.tile([P, 4, 1024], BF16, tag="raw_" + split[0])
+            view = src[i * 512 : (i + 1) * 512, :].rearrange("(b p) k -> p b k", p=P)
+            if split[1]:
+                for b in range(4):
+                    nc.sync.dma_start(out=raw_t[:, b, :], in_=view[:, b, :])
+            else:
+                nc.sync.dma_start(out=raw_t[:], in_=view)
+            store[i] = raw_t
+
+        def load_x(q):
+            xr = xraw_pool.tile([P, 2, 1024], BF16)
+            nc.sync.dma_start(
+                out=xr[:], in_=x[q * 256 : (q + 1) * 256, :].rearrange("(b p) k -> p b k", p=P)
+            )
+            x_raw[q] = xr
+
+        load_cls(rho_raw, rho, 0, ("r", True))
+        for q in range(4):
+            load_x(q)
+        load_cls(mean_raw, mean, 0, ("m", False))
+        load_cls(rho_raw, rho, 1, ("r", False))
+        load_cls(mean_raw, mean, 1, ("m", False))
+
+        ident = consts.tile([P, P], F32)
+        make_identity(nc, ident[:])
+        half = consts.tile([P, P], F32)
+        nc.vector.memset(half[:], 0.5)
+        one_col = consts.tile([P, 1], F32)
+        nc.vector.memset(one_col[:], 1.0)
+
+        xq = xkeep.tile([P, NB, 256], U32, align_bytes=64)
+        xs = xkeep.tile([P, NB, 256], U8, align_bytes=64)
+        x2q = xkeep.tile([P, NB, 256], U32, align_bytes=64)
+        x2s = xkeep.tile([P, NB, 256], U8, align_bytes=64)
+
+        def unit(t, u):
+            g, h = divmod(u, 2)
+            return t[:, 2 * g : 2 * g + 2, h * 256 : (h + 1) * 256, :].rearrange(
+                "p u c e -> p u (c e)"
+            )
+
+        def rho_t(i, b):
+            pt = ps_tr.tile([P, 4, 128], F32)
+            words = rho_raw[i][:, b, :].bitcast(F32)
+            for j in range(4):
+                nc.tensor.transpose(pt[:, j, :], words[:, j * 128 : (j + 1) * 128], ident[:])
+            rts[(i, b)] = pt
+
+        def act_a(i, b):
+            nc.scalar.activation(
+                out=chain[i][:, :, b * 128 : (b + 1) * 128, :].rearrange("p j c e -> p j (c e)"),
+                in_=rts[(i, b)][:].bitcast(BF16),
+                func=ACT.Exp,
+            )
+
+        def act_l(i):
+            halves = [
+                chain[i][:, 2 * g : 2 * g + 2, :, :].rearrange("p u c e -> p (u c e)")
+                for g in range(2)
+            ]
+            for hv in halves:
+                nc.scalar.activation(out=hv, in_=hv, func=ACT.Ln, bias=one_col[:])
+            for hv in halves:
+                nc.scalar.activation(out=hv, in_=hv, func=ACT.Ln)
+
+        def act_d(i, u):
+            nc.scalar.activation(out=unit(chain[i], u), in_=unit(chain[i], u), func=ACT.Exp, scale=-2.0)
+
+        def mean_t(i, u):
+            g, h = divmod(u, 2)
+            pm = ps_mt.tile([P, 2, 256], F32, tag="mt")
+            for uu in range(2):
+                for cb in range(2):
+                    words = mean_raw[i][:, 2 * h + cb, :].bitcast(F32)
+                    j = 2 * g + uu
+                    nc.tensor.transpose(
+                        pm[:, uu, cb * 128 : (cb + 1) * 128],
+                        words[:, j * 128 : (j + 1) * 128],
+                        ident[:],
+                    )
+            mts[(i, u)] = pm
+
+        def dve_t(i, u):
+            nc.vector.tensor_tensor(
+                out=unit(tprod[i], u), in0=mts[(i, u)][:].bitcast(BF16), in1=unit(chain[i], u), op=ALU.mult
+            )
+
+        def dve_v(i, u):
+            nc.vector.tensor_tensor(
+                out=unit(vprod[i], u), in0=mts[(i, u)][:].bitcast(BF16), in1=unit(tprod[i], u), op=ALU.mult
+            )
+
+        def cast(dst, src, g, factor):
+            nc.gpsimd.tensor_scalar(
+                out=dst[:, g, :, :].rearrange("p c (u e) -> p c u e", u=2),
+                in0=src[:, 2 * g : 2 * g + 2, :, :].rearrange("p u c e -> p c u e"),
+                scalar1=factor,
+                scalar2=0.0,
+                op0=ALU.mult,
+                op1=ALU.add,
+            )
+
+        def quant(src, q_t, s_t, g):
+            nc.vector.quantize_mx(
+                out=q_t[:, g, :].bitcast(FP8X4),
+                scales=s_t[:, g, :],
+                in_=src[:, g, :, :].rearrange("p c t -> p (c t)"),
+            )
+
+        def ones_mm(i, h):
+            acc_s = ps_s.tile([P, 512], F32)
+            for j in range(4):
+                nc.tensor.matmul(
+                    out=acc_s[:],
+                    lhsT=half[:],
+                    rhs=vprod[i][:, j, h * 256 : (h + 1) * 256, :].rearrange("p c e -> p (c e)"),
+                    start=(j == 0),
+                    stop=(j == 3),
+                )
+            return acc_s
+
+        def evac_s(i, h, acc_s):
+            nc.vector.tensor_reduce(
+                out=sb[i][:, h * 256 : (h + 1) * 256],
+                in_=acc_s[:].rearrange("p (c e) -> p c e", e=2),
+                axis=mybir.AxisListType.X,
+                op=ALU.add,
+            )
+
+        def mx_tile(i, bt):
+            wq, ws, mq, ms = cw[i]
+            acc = ps_mx.tile([P, 512], F32)
+            ops = []
+            for g in range(2):
+                ops.append((x2q, x2s, wq, ws, g))
+                ops.append((xq, xs, mq, ms, g))
+            for n, (lq, ls, rq, rs, g) in enumerate(ops):
+                nc.tensor.matmul_mx(
+                    out=acc[:],
+                    lhsT=lq[:, bt, g * 128 : (g + 1) * 128].bitcast(FP8X4),
+                    lhsT_scale=ls[:, bt, g * 128 : (g + 1) * 128],
+                    rhs=rq[:, g, :].bitcast(FP8X4),
+                    rhs_scale=rs[:, g, :],
+                    start=(n == 0),
+                    stop=(n == 3),
+                )
+            nc.vector.tensor_tensor(out=pre[i][:, bt, :], in0=acc[:], in1=sb[i][:], op=ALU.add)
+
+        def final(i, b0, nb):
+            sl = pre[i][:, b0 : b0 + nb, :]
+            nc.scalar.activation(out=sl, in_=sl, func=ACT.Exp, scale=-1.0)
+            nc.sync.dma_start(
+                out=out[b0 * P : (b0 + nb) * P, i * 512 : (i + 1) * 512].rearrange(
+                    "(t p) c -> p t c", p=P
+                ),
+                in_=sl,
+            )
+
+        chain0 = chain_pool.tile([P, 4, 512, 2], F32, tag="chain")
+        chain[0] = chain0
+        rho_t(0, 0)
+        rho_t(0, 1)
+        act_a(0, 0)
+        rho_t(0, 2)
+        act_a(0, 1)
+        rho_t(0, 3)
+        act_a(0, 2)
+        act_a(0, 3)
+        act_l(0)
+
+        xgs = {}
+
+        def x_quant(bt):
+            xg, x2g = xgs[bt]
+            nc.vector.quantize_mx(
+                out=xq[:, bt, :].bitcast(FP8X4), scales=xs[:, bt, :],
+                in_=xg[:].rearrange("p g b t -> p (g b t)"),
+            )
+            nc.vector.quantize_mx(
+                out=x2q[:, bt, :].bitcast(FP8X4), scales=x2s[:, bt, :],
+                in_=x2g[:].rearrange("p g b t -> p (g b t)"),
+            )
+
+        for bt in range(NB):
+            px = ps_mt.tile([P, 4, 128], F32, tag="mt")
+            words = x_raw[bt // 2][:, bt % 2, :].bitcast(F32)
+            for j in range(4):
+                nc.tensor.transpose(px[:, j, :], words[:, j * 128 : (j + 1) * 128], ident[:])
+            xg = xstage.tile([P, 2, 128, 4], BF16, align_bytes=64)
+            nc.vector.tensor_copy(
+                out=xg[:].bitcast(F32), in_=px[:].rearrange("p (g u) b -> p g b u", g=2)
+            )
+            x2g = xstage.tile([P, 2, 128, 4], BF16, align_bytes=64)
+            nc.vector.tensor_tensor(out=x2g[:], in0=xg[:], in1=xg[:], op=ALU.mult)
+            xgs[bt] = (xg, x2g)
+            if bt > 0:
+                x_quant(bt - 1)
+        x_quant(NB - 1)
+
+        mean_t(0, 0)
+        mean_t(0, 1)
+        rho_t(1, 0)
+        rho_t(1, 1)
+
+        for i in range(NCH):
+            tp = work.tile([P, 4, 512, 2], F32)
+            tprod[i] = tp
+            vp = work.tile([P, 4, 512, 2], F32)
+            vprod[i] = vp
+            wgt = work.tile([P, 2, 512, 4], BF16, align_bytes=64)
+            wg[i] = wgt
+            mwgt = work.tile([P, 2, 512, 4], BF16, align_bytes=64)
+            mwg[i] = mwgt
+            wq = codes.tile([P, 2, 512], U32, align_bytes=64)
+            ws = codes.tile([P, 2, 512], U8, align_bytes=64)
+            mq = codes.tile([P, 2, 512], U32, align_bytes=64)
+            ms = codes.tile([P, 2, 512], U8, align_bytes=64)
+            cw[i] = (wq, ws, mq, ms)
+            sbt = codes.tile([P, 512], F32)
+            sb[i] = sbt
+
+            act_d(i, 0)
+            act_d(i, 1)
+            dve_t(i, 0)
+            dve_t(i, 1)
+            cast(wg[i], chain[i], 0, 0.5)
+            act_d(i, 2)
+            act_d(i, 3)
+            dve_v(i, 0)
+            mean_t(i, 2)
+            dve_v(i, 1)
+            mean_t(i, 3)
+            cast(mwg[i], tprod[i], 0, -1.0)
+            dve_t(i, 2)
+            dve_t(i, 3)
+            cast(wg[i], chain[i], 1, 0.5)
+            dve_v(i, 2)
+            dve_v(i, 3)
+            cast(mwg[i], tprod[i], 1, -1.0)
+            if i + 1 < NCH:
+                chain_n = chain_pool.tile([P, 4, 512, 2], F32, tag="chain")
+                chain[i + 1] = chain_n
+                act_a(i + 1, 0)
+                rho_t(i + 1, 2)
+                act_a(i + 1, 1)
+                rho_t(i + 1, 3)
+                act_a(i + 1, 2)
+                act_a(i + 1, 3)
+                act_l(i + 1)
+            if i + 2 < NCH:
+                load_cls(rho_raw, rho, i + 2, ("r", False))
+                load_cls(mean_raw, mean, i + 2, ("m", False))
+            acc0 = ones_mm(i, 0)
+            acc1 = ones_mm(i, 1)
+            if i + 1 < NCH:
+                mean_t(i + 1, 0)
+                mean_t(i + 1, 1)
+            if i + 2 < NCH:
+                rho_t(i + 2, 0)
+                rho_t(i + 2, 1)
+            quant(wg[i], wq, ws, 0)
+            quant(mwg[i], mq, ms, 0)
+            quant(wg[i], wq, ws, 1)
+            quant(mwg[i], mq, ms, 1)
+            evac_s(i, 0, acc0)
+            evac_s(i, 1, acc1)
+            if i == NCH - 1:
+                for b0 in range(0, NB, 2):
+                    final(0, b0, 2)
+            pre_t = pre_pool.tile([P, NB, 512], F32)
+            pre[i] = pre_t
+            for bt in range(NB):
+                mx_tile(i, bt)
+
+        for i in range(1, NCH):
+            for b0 in range(0, NB, 2):
+                final(i, b0, 2)

@@ -29,10 +29,10 @@ def tile_dynamic_estimator_kernel(tc, x, mean, rho, out):
         work = ctx.enter_context(tc.tile_pool(name="work", bufs=1))
         codes = ctx.enter_context(tc.tile_pool(name="codes", bufs=2))
         pre_pool = ctx.enter_context(tc.tile_pool(name="pre", bufs=3))
-        ps_tr = ctx.enter_context(tc.psum_pool(name="ps_tr", bufs=2))
+        ps_tr = ctx.enter_context(tc.psum_pool(name="ps_tr", bufs=3))
         ps_mt = ctx.enter_context(tc.psum_pool(name="ps_mt", bufs=2))
-        ps_s = ctx.enter_context(tc.psum_pool(name="ps_s", bufs=2))
-        ps_mx = ctx.enter_context(tc.psum_pool(name="ps_mx", bufs=2))
+        ps_acc = ctx.enter_context(tc.psum_pool(name="ps_acc", bufs=3))
+        ctx.enter_context(tc.manual_schedule())
 
         rho_raw = {}
         mean_raw = {}
@@ -47,6 +47,8 @@ def tile_dynamic_estimator_kernel(tc, x, mean, rho, out):
         pre = {}
         rts = {}
         mts = {}
+        saccs = {}
+        accs = {}
 
         def load_cls(store, src, i, split):
             raw_t = raw_pool.tile([P, 4, 1024], BF16, tag="raw_" + split[0])
@@ -68,8 +70,8 @@ def tile_dynamic_estimator_kernel(tc, x, mean, rho, out):
         load_cls(rho_raw, rho, 0, ("r", True))
         for q in range(4):
             load_x(q)
-        load_cls(mean_raw, mean, 0, ("m", False))
         load_cls(rho_raw, rho, 1, ("r", False))
+        load_cls(mean_raw, mean, 0, ("m", False))
         load_cls(mean_raw, mean, 1, ("m", False))
 
         ident = consts.tile([P, P], F32)
@@ -158,29 +160,31 @@ def tile_dynamic_estimator_kernel(tc, x, mean, rho, out):
                 in_=src[:, g, :, :].rearrange("p c t -> p (c t)"),
             )
 
-        def ones_mm(i, h):
-            acc_s = ps_s.tile([P, 512], F32)
-            for j in range(4):
+        def ones_mm(i, h, g):
+            if g == 0:
+                acc_s = ps_acc.tile([P, 512], F32, tag="acc")
+                saccs[(i, h)] = acc_s
+            for j in (2 * g, 2 * g + 1):
                 nc.tensor.matmul(
-                    out=acc_s[:],
+                    out=saccs[(i, h)][:],
                     lhsT=half[:],
                     rhs=vprod[i][:, j, h * 256 : (h + 1) * 256, :].rearrange("p c e -> p (c e)"),
                     start=(j == 0),
                     stop=(j == 3),
                 )
-            return acc_s
 
-        def evac_s(i, h, acc_s):
+        def evac_s(i, h):
             nc.vector.tensor_reduce(
                 out=sb[i][:, h * 256 : (h + 1) * 256],
-                in_=acc_s[:].rearrange("p (c e) -> p c e", e=2),
+                in_=saccs[(i, h)][:].rearrange("p (c e) -> p c e", e=2),
                 axis=mybir.AxisListType.X,
                 op=ALU.add,
             )
 
         def mx_tile(i, bt):
             wq, ws, mq, ms = cw[i]
-            acc = ps_mx.tile([P, 512], F32)
+            acc = ps_acc.tile([P, 512], F32, tag="acc")
+            accs[(i, bt)] = acc
             ops = []
             for g in range(2):
                 ops.append((x2q, x2s, wq, ws, g))
@@ -195,7 +199,14 @@ def tile_dynamic_estimator_kernel(tc, x, mean, rho, out):
                     start=(n == 0),
                     stop=(n == 3),
                 )
-            nc.vector.tensor_tensor(out=pre[i][:, bt, :], in0=acc[:], in1=sb[i][:], op=ALU.add)
+
+        def add_s(i, bt):
+            if bt == 0:
+                pre_t = pre_pool.tile([P, NB, 512], F32)
+                pre[i] = pre_t
+            nc.vector.tensor_tensor(
+                out=pre[i][:, bt, :], in0=accs[(i, bt)][:], in1=sb[i][:], op=ALU.add
+            )
 
         def final(i, b0, nb):
             sl = pre[i][:, b0 : b0 + nb, :]
@@ -211,10 +222,10 @@ def tile_dynamic_estimator_kernel(tc, x, mean, rho, out):
         chain[0] = chain0
         rho_t(0, 0)
         rho_t(0, 1)
-        act_a(0, 0)
         rho_t(0, 2)
-        act_a(0, 1)
+        act_a(0, 0)
         rho_t(0, 3)
+        act_a(0, 1)
         act_a(0, 2)
         act_a(0, 3)
         act_l(0)
@@ -246,12 +257,14 @@ def tile_dynamic_estimator_kernel(tc, x, mean, rho, out):
             xgs[bt] = (xg, x2g)
             if bt > 0:
                 x_quant(bt - 1)
+            if bt == 4:
+                rho_t(1, 0)
+                rho_t(1, 1)
+                rho_t(1, 2)
         x_quant(NB - 1)
 
         mean_t(0, 0)
         mean_t(0, 1)
-        rho_t(1, 0)
-        rho_t(1, 1)
 
         for i in range(NCH):
             tp = work.tile([P, 4, 512, 2], F32)
@@ -270,58 +283,83 @@ def tile_dynamic_estimator_kernel(tc, x, mean, rho, out):
             sbt = codes.tile([P, 512], F32)
             sb[i] = sbt
 
-            act_d(i, 0)
-            act_d(i, 1)
-            dve_t(i, 0)
-            dve_t(i, 1)
-            cast(wg[i], chain[i], 0, 0.5)
-            act_d(i, 2)
-            act_d(i, 3)
-            dve_v(i, 0)
-            mean_t(i, 2)
-            dve_v(i, 1)
-            mean_t(i, 3)
-            cast(mwg[i], tprod[i], 0, -1.0)
-            dve_t(i, 2)
-            dve_t(i, 3)
-            cast(wg[i], chain[i], 1, 0.5)
-            dve_v(i, 2)
-            dve_v(i, 3)
-            cast(mwg[i], tprod[i], 1, -1.0)
-            if i + 1 < NCH:
+            late = {"add": 0, "mx": 3}
+
+            def adds_of_last_chunk(n):
+                for q in range(n):
+                    if i > 0 and late["add"] < NB:
+                        add_s(i - 1, late["add"])
+                        late["add"] = late["add"] + 1
+                        if late["mx"] < NB:
+                            mx_tile(i - 1, late["mx"])
+                            late["mx"] = late["mx"] + 1
+
+            nxt = i + 1 < NCH
+            nxt2 = i + 2 < NCH
+            for u in range(4):
+                act_d(i, u)
+            if nxt:
                 chain_n = chain_pool.tile([P, 4, 512, 2], F32, tag="chain")
                 chain[i + 1] = chain_n
                 act_a(i + 1, 0)
-                rho_t(i + 1, 2)
                 act_a(i + 1, 1)
-                rho_t(i + 1, 3)
                 act_a(i + 1, 2)
+            if nxt2:
+                load_cls(rho_raw, rho, i + 2, ("r", False))
+            adds_of_last_chunk(2)
+            dve_t(i, 0)
+            adds_of_last_chunk(1)
+            dve_t(i, 1)
+            cast(wg[i], chain[i], 0, 0.5)
+            adds_of_last_chunk(1)
+            if nxt:
+                rho_t(i + 1, 3)
                 act_a(i + 1, 3)
                 act_l(i + 1)
-            if i + 2 < NCH:
-                load_cls(rho_raw, rho, i + 2, ("r", False))
-                load_cls(mean_raw, mean, i + 2, ("m", False))
-            acc0 = ones_mm(i, 0)
-            acc1 = ones_mm(i, 1)
-            if i + 1 < NCH:
-                mean_t(i + 1, 0)
-                mean_t(i + 1, 1)
-            if i + 2 < NCH:
+            dve_v(i, 0)
+            if nxt2:
                 rho_t(i + 2, 0)
+            mean_t(i, 2)
+            adds_of_last_chunk(1)
+            dve_v(i, 1)
+            adds_of_last_chunk(NB)
+            if nxt2:
                 rho_t(i + 2, 1)
+            ones_mm(i, 0, 0)
+            mean_t(i, 3)
+            if nxt2:
+                rho_t(i + 2, 2)
+            cast(mwg[i], tprod[i], 0, -1.0)
+            cast(wg[i], chain[i], 1, 0.5)
+            if nxt2:
+                load_cls(mean_raw, mean, i + 2, ("m", False))
+            dve_t(i, 2)
+            dve_v(i, 2)
+            if nxt:
+                mean_t(i + 1, 0)
+            dve_t(i, 3)
+            cast(mwg[i], tprod[i], 1, -1.0)
+            dve_v(i, 3)
+            ones_mm(i, 0, 1)
+            if nxt:
+                mean_t(i + 1, 1)
+            ones_mm(i, 1, 0)
+            ones_mm(i, 1, 1)
             quant(wg[i], wq, ws, 0)
             quant(mwg[i], mq, ms, 0)
             quant(wg[i], wq, ws, 1)
+            evac_s(i, 0)
             quant(mwg[i], mq, ms, 1)
-            evac_s(i, 0, acc0)
-            evac_s(i, 1, acc1)
-            if i == NCH - 1:
+            evac_s(i, 1)
+            if nxt:
+                for bt in range(3):
+                    mx_tile(i, bt)
+            else:
                 for b0 in range(0, NB, 2):
                     final(0, b0, 2)
-            pre_t = pre_pool.tile([P, NB, 512], F32)
-            pre[i] = pre_t
-            for bt in range(NB):
-                mx_tile(i, bt)
+                for bt in range(NB):
+                    mx_tile(i, bt)
+                    add_s(i, bt)
 
         for i in range(1, NCH):
             for b0 in range(0, NB, 2):

@@ -361,6 +361,8 @@ def tile_dynamic_estimator_kernel(tc, x, mean, rho, out):
                     mx_tile(i, bt)
                     add_s(i, bt)
 
-        for i in range(1, NCH):
+        for i in range(1, NCH - 1):
             for b0 in range(0, NB, 2):
                 final(i, b0, 2)
+        for b0 in range(NB):
+            final(NCH - 1, b0, 1)

@@ -7,7 +7,11 @@ FLOPS = 2 * 2 * 1024 * 2048 * 1024
 
 P = 128
 NB = 8
-NCH = 4
+NU = 8
+UC = 256
+X2_G = range(8)
+RS = False
+GROUPS = [[0, 1, 2], [3, 4, 5], [6, 7]]
 F32 = mybir.dt.float32
 BF16 = mybir.dt.bfloat16
 U32 = mybir.dt.uint32
@@ -21,17 +25,18 @@ def tile_dynamic_estimator_kernel(tc, x, mean, rho, out):
     nc = tc.nc
     with ExitStack() as ctx:
         consts = ctx.enter_context(tc.tile_pool(name="consts", bufs=1))
-        xraw_pool = ctx.enter_context(tc.tile_pool(name="xraw", bufs=4))
-        xstage = ctx.enter_context(tc.tile_pool(name="xstage", bufs=2))
+        xraw_pool = ctx.enter_context(tc.tile_pool(name="xraw", bufs=2))
+        xstage = ctx.enter_context(tc.tile_pool(name="xstage", bufs=4))
         xkeep = ctx.enter_context(tc.tile_pool(name="xkeep", bufs=1))
-        raw_pool = ctx.enter_context(tc.tile_pool(name="raw", bufs=2))
-        chain_pool = ctx.enter_context(tc.tile_pool(name="chain", bufs=2))
-        work = ctx.enter_context(tc.tile_pool(name="work", bufs=1))
+        rho_pool = ctx.enter_context(tc.tile_pool(name="rho", bufs=5))
+        mean_pool = ctx.enter_context(tc.tile_pool(name="mean", bufs=3))
+        chain_pool = ctx.enter_context(tc.tile_pool(name="chain", bufs=6))
+        work = ctx.enter_context(tc.tile_pool(name="work", bufs=2))
         codes = ctx.enter_context(tc.tile_pool(name="codes", bufs=2))
-        pre_pool = ctx.enter_context(tc.tile_pool(name="pre", bufs=3))
-        ps_tr = ctx.enter_context(tc.psum_pool(name="ps_tr", bufs=3))
-        ps_mt = ctx.enter_context(tc.psum_pool(name="ps_mt", bufs=2))
-        ps_acc = ctx.enter_context(tc.psum_pool(name="ps_acc", bufs=3))
+        pre_pool = ctx.enter_context(tc.tile_pool(name="pre", bufs=5))
+        ps_rho = ctx.enter_context(tc.psum_pool(name="ps_rho", bufs=2))
+        ps_mean = ctx.enter_context(tc.psum_pool(name="ps_mean", bufs=2))
+        ps_acc = ctx.enter_context(tc.psum_pool(name="ps_acc", bufs=4))
         ctx.enter_context(tc.manual_schedule())
 
         rho_raw = {}
@@ -40,6 +45,7 @@ def tile_dynamic_estimator_kernel(tc, x, mean, rho, out):
         chain = {}
         tprod = {}
         vprod = {}
+        vsum = {}
         wg = {}
         mwg = {}
         cw = {}
@@ -47,18 +53,22 @@ def tile_dynamic_estimator_kernel(tc, x, mean, rho, out):
         pre = {}
         rts = {}
         mts = {}
-        saccs = {}
+        ssum = {}
         accs = {}
 
-        def load_cls(store, src, i, split):
-            raw_t = raw_pool.tile([P, 4, 1024], BF16, tag="raw_" + split[0])
-            view = src[i * 512 : (i + 1) * 512, :].rearrange("(b p) k -> p b k", p=P)
-            if split[1]:
-                for b in range(4):
-                    nc.sync.dma_start(out=raw_t[:, b, :], in_=view[:, b, :])
-            else:
-                nc.sync.dma_start(out=raw_t[:], in_=view)
-            store[i] = raw_t
+        def load_rho(u):
+            rr = rho_pool.tile([P, 2, 1024], BF16)
+            nc.sync.dma_start(
+                out=rr[:], in_=rho[u * UC : (u + 1) * UC, :].rearrange("(b p) k -> p b k", p=P)
+            )
+            rho_raw[u] = rr
+
+        def load_mean(u):
+            mr = mean_pool.tile([P, 2, 1024], BF16)
+            nc.sync.dma_start(
+                out=mr[:], in_=mean[u * UC : (u + 1) * UC, :].rearrange("(b p) k -> p b k", p=P)
+            )
+            mean_raw[u] = mr
 
         def load_x(q):
             xr = xraw_pool.tile([P, 2, 1024], BF16)
@@ -67,12 +77,18 @@ def tile_dynamic_estimator_kernel(tc, x, mean, rho, out):
             )
             x_raw[q] = xr
 
-        load_cls(rho_raw, rho, 0, ("r", True))
-        for q in range(4):
+        load_rho(0)
+        load_x(0)
+        load_rho(1)
+        load_x(1)
+        load_rho(2)
+        for q in range(2, 4):
             load_x(q)
-        load_cls(rho_raw, rho, 1, ("r", False))
-        load_cls(mean_raw, mean, 0, ("m", False))
-        load_cls(mean_raw, mean, 1, ("m", False))
+        load_mean(0)
+        load_rho(3)
+        load_mean(1)
+        load_rho(4)
+        load_mean(2)
 
         ident = consts.tile([P, P], F32)
         make_identity(nc, ident[:])
@@ -86,61 +102,76 @@ def tile_dynamic_estimator_kernel(tc, x, mean, rho, out):
         x2q = xkeep.tile([P, NB, 256], U32, align_bytes=64)
         x2s = xkeep.tile([P, NB, 256], U8, align_bytes=64)
 
-        def unit(t, u):
-            g, h = divmod(u, 2)
-            return t[:, 2 * g : 2 * g + 2, h * 256 : (h + 1) * 256, :].rearrange(
-                "p u c e -> p u (c e)"
-            )
+        def part(t, g):
+            return t[:, 2 * g : 2 * g + 2, :, :].rearrange("p u c e -> p u (c e)")
 
-        def rho_t(i, b):
-            pt = ps_tr.tile([P, 4, 128], F32)
-            words = rho_raw[i][:, b, :].bitcast(F32)
+        def rho_t(u, b, spare=False):
+            if spare:
+                pt = ps_acc.tile([P, 4, 128], F32, tag="acc")
+            else:
+                pt = ps_rho.tile([P, 4, 128], F32, tag="rho")
+            words = rho_raw[u][:, b, :].bitcast(F32)
             for j in range(4):
                 nc.tensor.transpose(pt[:, j, :], words[:, j * 128 : (j + 1) * 128], ident[:])
-            rts[(i, b)] = pt
+            rts[(u, b)] = pt
 
-        def act_a(i, b):
+        def act_a(u, b):
+            if b == 0:
+                ch = chain_pool.tile([P, 4, UC, 2], F32)
+                chain[u] = ch
             nc.scalar.activation(
-                out=chain[i][:, :, b * 128 : (b + 1) * 128, :].rearrange("p j c e -> p j (c e)"),
-                in_=rts[(i, b)][:].bitcast(BF16),
+                out=chain[u][:, :, b * 128 : (b + 1) * 128, :].rearrange("p j c e -> p j (c e)"),
+                in_=rts[(u, b)][:].bitcast(BF16),
                 func=ACT.Exp,
             )
 
-        def act_l(i):
-            halves = [
-                chain[i][:, 2 * g : 2 * g + 2, :, :].rearrange("p u c e -> p (u c e)")
-                for g in range(2)
-            ]
-            for hv in halves:
-                nc.scalar.activation(out=hv, in_=hv, func=ACT.Ln, bias=one_col[:])
-            for hv in halves:
-                nc.scalar.activation(out=hv, in_=hv, func=ACT.Ln)
+        def flat(t):
+            return t[:].rearrange("p u c e -> p (u c e)")
 
-        def act_d(i, u):
-            nc.scalar.activation(out=unit(chain[i], u), in_=unit(chain[i], u), func=ACT.Exp, scale=-2.0)
+        def act_l(units):
+            for u in units:
+                nc.scalar.activation(out=flat(chain[u]), in_=flat(chain[u]), func=ACT.Ln, bias=one_col[:])
+            for u in units:
+                nc.scalar.activation(out=flat(chain[u]), in_=flat(chain[u]), func=ACT.Ln)
 
-        def mean_t(i, u):
-            g, h = divmod(u, 2)
-            pm = ps_mt.tile([P, 2, 256], F32, tag="mt")
+        def act_d(u):
+            for g in range(2):
+                nc.scalar.activation(
+                    out=part(chain[u], g), in_=part(chain[u], g), func=ACT.Exp, scale=-2.0
+                )
+
+        def mean_t(u, g):
+            pm = ps_mean.tile([P, 2, 256], F32, tag="mean")
             for uu in range(2):
                 for cb in range(2):
-                    words = mean_raw[i][:, 2 * h + cb, :].bitcast(F32)
+                    words = mean_raw[u][:, cb, :].bitcast(F32)
                     j = 2 * g + uu
                     nc.tensor.transpose(
-                        pm[:, uu, cb * 128 : (cb + 1) * 128],
-                        words[:, j * 128 : (j + 1) * 128],
-                        ident[:],
+                        pm[:, uu, cb * 128 : (cb + 1) * 128], words[:, j * 128 : (j + 1) * 128], ident[:]
                     )
-            mts[(i, u)] = pm
+            mts[(u, g)] = pm
 
-        def dve_t(i, u):
+        def dve_t(u, g):
+            if g == 0:
+                tp = work.tile([P, 4, UC, 2], F32)
+                tprod[u] = tp
             nc.vector.tensor_tensor(
-                out=unit(tprod[i], u), in0=mts[(i, u)][:].bitcast(BF16), in1=unit(chain[i], u), op=ALU.mult
+                out=part(tprod[u], g), in0=mts[(u, g)][:].bitcast(BF16), in1=part(chain[u], g), op=ALU.mult
             )
 
-        def dve_v(i, u):
+        def dve_v(u, g):
+            if g == 0:
+                vp = work.tile([P, 4, UC, 2], F32)
+                vprod[u] = vp
             nc.vector.tensor_tensor(
-                out=unit(vprod[i], u), in0=mts[(i, u)][:].bitcast(BF16), in1=unit(tprod[i], u), op=ALU.mult
+                out=part(vprod[u], g), in0=mts[(u, g)][:].bitcast(BF16), in1=part(tprod[u], g), op=ALU.mult
+            )
+
+        def add_v(u):
+            vs = work.tile([P, 2, UC, 2], F32)
+            vsum[u] = vs
+            nc.gpsimd.tensor_tensor(
+                out=flat(vs), in0=part(vprod[u], 0), in1=part(vprod[u], 1), op=ALU.add
             )
 
         def cast(dst, src, g, factor):
@@ -153,98 +184,102 @@ def tile_dynamic_estimator_kernel(tc, x, mean, rho, out):
                 op1=ALU.add,
             )
 
-        def quant(src, q_t, s_t, g):
-            nc.vector.quantize_mx(
-                out=q_t[:, g, :].bitcast(FP8X4),
-                scales=s_t[:, g, :],
-                in_=src[:, g, :, :].rearrange("p c t -> p (c t)"),
-            )
-
-        def ones_mm(i, h, g):
-            if g == 0:
-                acc_s = ps_acc.tile([P, 512], F32, tag="acc")
-                saccs[(i, h)] = acc_s
-            for j in (2 * g, 2 * g + 1):
-                nc.tensor.matmul(
-                    out=saccs[(i, h)][:],
-                    lhsT=half[:],
-                    rhs=vprod[i][:, j, h * 256 : (h + 1) * 256, :].rearrange("p c e -> p (c e)"),
-                    start=(j == 0),
-                    stop=(j == 3),
-                )
-
-        def evac_s(i, h):
-            nc.vector.tensor_reduce(
-                out=sb[i][:, h * 256 : (h + 1) * 256],
-                in_=saccs[(i, h)][:].rearrange("p (c e) -> p c e", e=2),
-                axis=mybir.AxisListType.X,
-                op=ALU.add,
-            )
-
-        def mx_tile(i, bt):
-            wq, ws, mq, ms = cw[i]
-            acc = ps_acc.tile([P, 512], F32, tag="acc")
-            accs[(i, bt)] = acc
-            ops = []
+        def cast_w(u):
+            wgt = work.tile([P, 2, UC, 4], BF16, align_bytes=64)
+            wg[u] = wgt
             for g in range(2):
-                ops.append((x2q, x2s, wq, ws, g))
-                ops.append((xq, xs, mq, ms, g))
-            for n, (lq, ls, rq, rs, g) in enumerate(ops):
-                nc.tensor.matmul_mx(
-                    out=acc[:],
-                    lhsT=lq[:, bt, g * 128 : (g + 1) * 128].bitcast(FP8X4),
-                    lhsT_scale=ls[:, bt, g * 128 : (g + 1) * 128],
-                    rhs=rq[:, g, :].bitcast(FP8X4),
-                    rhs_scale=rs[:, g, :],
+                cast(wgt, chain[u], g, 0.5)
+
+        def cast_mw(u, g):
+            if g == 0:
+                mwgt = work.tile([P, 2, UC, 4], BF16, align_bytes=64)
+                mwg[u] = mwgt
+            cast(mwg[u], tprod[u], g, -1.0)
+
+        def quant(src, q_t, s_t):
+            nc.vector.quantize_mx(
+                out=q_t[:].rearrange("p g c -> p (g c)").bitcast(FP8X4),
+                scales=s_t[:].rearrange("p g c -> p (g c)"),
+                in_=src[:].rearrange("p g c t -> p (g c t)"),
+            )
+
+        def quant_w(u):
+            wq = codes.tile([P, 2, UC], U32, align_bytes=64)
+            ws = codes.tile([P, 2, UC], U8, align_bytes=64)
+            cw[(u, 0)] = (wq, ws)
+            quant(wg[u], wq, ws)
+
+        def quant_mw(u):
+            mq = codes.tile([P, 2, UC], U32, align_bytes=64)
+            ms = codes.tile([P, 2, UC], U8, align_bytes=64)
+            cw[(u, 1)] = (mq, ms)
+            quant(mwg[u], mq, ms)
+
+        def ones_mm(u):
+            ss = ps_acc.tile([P, UC], F32, tag="acc")
+            ssum[u] = ss
+            for n in range(4):
+                uu, e = divmod(n, 2)
+                nc.tensor.matmul(
+                    out=ss[:],
+                    lhsT=half[:],
+                    rhs=vsum[u][:, uu, :, e],
                     start=(n == 0),
                     stop=(n == 3),
                 )
 
-        def add_s(i, bt):
-            if bt == 0:
-                pre_t = pre_pool.tile([P, NB, 512], F32)
-                pre[i] = pre_t
+        def evac_s(u):
+            sbt = codes.tile([P, UC], F32)
+            sb[u] = sbt
+            nc.vector.tensor_copy(out=sbt[:], in_=ssum[u][:])
+
+        def mx_pair(u, q):
+            acc = ps_acc.tile([P, 2, UC], F32, tag="acc")
+            accs[(u, q)] = acc
+            wq, ws = cw[(u, 0)]
+            mq, ms = cw[(u, 1)]
+            for r in range(2):
+                bt = 2 * q + r
+                ops = []
+                for g in range(2):
+                    ops.append((x2q, x2s, wq, ws, g))
+                    ops.append((xq, xs, mq, ms, g))
+                for n, (lq, ls, rq, rs, g) in enumerate(ops):
+                    nc.tensor.matmul_mx(
+                        out=acc[:, r, :],
+                        lhsT=lq[:, bt, g * 128 : (g + 1) * 128].bitcast(FP8X4),
+                        lhsT_scale=ls[:, bt, g * 128 : (g + 1) * 128],
+                        rhs=rq[:, g, :].bitcast(FP8X4),
+                        rhs_scale=rs[:, g, :],
+                        start=(n == 0),
+                        stop=(n == 3),
+                    )
+
+        def add_s(u, q):
+            if q == 0:
+                pre_t = pre_pool.tile([P, NB, UC], F32)
+                pre[u] = pre_t
             nc.vector.tensor_tensor(
-                out=pre[i][:, bt, :], in0=accs[(i, bt)][:], in1=sb[i][:], op=ALU.add
+                out=pre[u][:, 2 * q : 2 * q + 2, :],
+                in0=accs[(u, q)][:],
+                in1=sb[u][:].unsqueeze(1).to_broadcast([P, 2, UC]),
+                op=ALU.add,
             )
 
-        def final(i, b0, nb):
-            sl = pre[i][:, b0 : b0 + nb, :]
+        def final(u, b0, nb):
+            sl = pre[u][:, b0 : b0 + nb, :]
             nc.scalar.activation(out=sl, in_=sl, func=ACT.Exp, scale=-1.0)
             nc.sync.dma_start(
-                out=out[b0 * P : (b0 + nb) * P, i * 512 : (i + 1) * 512].rearrange(
+                out=out[b0 * P : (b0 + nb) * P, u * UC : (u + 1) * UC].rearrange(
                     "(t p) c -> p t c", p=P
                 ),
                 in_=sl,
             )
 
-        chain0 = chain_pool.tile([P, 4, 512, 2], F32, tag="chain")
-        chain[0] = chain0
-        rho_t(0, 0)
-        rho_t(0, 1)
-        rho_t(0, 2)
-        act_a(0, 0)
-        rho_t(0, 3)
-        act_a(0, 1)
-        act_a(0, 2)
-        act_a(0, 3)
-        act_l(0)
-
         xgs = {}
 
-        def x_quant(bt):
-            xg, x2g = xgs[bt]
-            nc.vector.quantize_mx(
-                out=xq[:, bt, :].bitcast(FP8X4), scales=xs[:, bt, :],
-                in_=xg[:].rearrange("p g b t -> p (g b t)"),
-            )
-            nc.vector.quantize_mx(
-                out=x2q[:, bt, :].bitcast(FP8X4), scales=x2s[:, bt, :],
-                in_=x2g[:].rearrange("p g b t -> p (g b t)"),
-            )
-
-        for bt in range(NB):
-            px = ps_mt.tile([P, 4, 128], F32, tag="mt")
+        def x_turn(bt):
+            px = ps_mean.tile([P, 4, 128], F32, tag="mean")
             words = x_raw[bt // 2][:, bt % 2, :].bitcast(F32)
             for j in range(4):
                 nc.tensor.transpose(px[:, j, :], words[:, j * 128 : (j + 1) * 128], ident[:])
@@ -253,116 +288,152 @@ def tile_dynamic_estimator_kernel(tc, x, mean, rho, out):
                 out=xg[:].bitcast(F32), in_=px[:].rearrange("p (g u) b -> p g b u", g=2)
             )
             x2g = xstage.tile([P, 2, 128, 4], BF16, align_bytes=64)
-            nc.vector.tensor_tensor(out=x2g[:], in0=xg[:], in1=xg[:], op=ALU.mult)
+            eng = nc.gpsimd if bt in X2_G else nc.vector
+            eng.tensor_tensor(out=x2g[:], in0=xg[:], in1=xg[:], op=ALU.mult)
             xgs[bt] = (xg, x2g)
-            if bt > 0:
-                x_quant(bt - 1)
-            if bt == 4:
-                rho_t(1, 0)
-                rho_t(1, 1)
-                rho_t(1, 2)
-        x_quant(NB - 1)
 
+        def x_quant(bt, w):
+            q_t, s_t = ((xq, xs), (x2q, x2s))[w]
+            nc.vector.quantize_mx(
+                out=q_t[:, bt, :].bitcast(FP8X4), scales=s_t[:, bt, :],
+                in_=xgs[bt][w][:].rearrange("p g b t -> p (g b t)"),
+            )
+
+        def act_l1(u):
+            nc.scalar.activation(out=flat(chain[u]), in_=flat(chain[u]), func=ACT.Ln, bias=one_col[:])
+
+        def square(eng, u):
+            eng.tensor_tensor(out=flat(chain[u]), in0=flat(chain[u]), in1=flat(chain[u]), op=ALU.mult)
+
+        def act_r(u):
+            for g in range(2):
+                nc.scalar.activation(
+                    out=part(chain[u], g), in_=part(chain[u], g), func=ACT.Abs_reciprocal_sqrt
+                )
+
+        banks = [(u, b) for u in GROUPS[0] for b in range(2)]
+        rho_t(*banks[0])
+        rho_t(*banks[1])
+        for n in range(NB):
+            if n < len(banks):
+                act_a(*banks[n])
+            x_turn(n)
+            if n + 2 < len(banks):
+                rho_t(*banks[n + 2])
+            if n > 0:
+                x_quant(n - 1, 0)
+                x_quant(n - 1, 1)
+        for u in GROUPS[0]:
+            act_l1(u)
+        load_rho(5)
+        if RS:
+            square(nc.vector, 0)
+            square(nc.gpsimd, 1)
+            square(nc.vector, 0)
+            x_quant(7, 0)
+            x_quant(7, 1)
+            square(nc.vector, 1)
+            square(nc.vector, 2)
+            square(nc.vector, 2)
+            for u in GROUPS[0]:
+                act_r(u)
+        else:
+            for u in GROUPS[0]:
+                nc.scalar.activation(out=flat(chain[u]), in_=flat(chain[u]), func=ACT.Ln)
+            x_quant(7, 0)
+            x_quant(7, 1)
+            for u in GROUPS[0]:
+                act_d(u)
         mean_t(0, 0)
         mean_t(0, 1)
 
-        for i in range(NCH):
-            tp = work.tile([P, 4, 512, 2], F32)
-            tprod[i] = tp
-            vp = work.tile([P, 4, 512, 2], F32)
-            vprod[i] = vp
-            wgt = work.tile([P, 2, 512, 4], BF16, align_bytes=64)
-            wg[i] = wgt
-            mwgt = work.tile([P, 2, 512, 4], BF16, align_bytes=64)
-            mwg[i] = mwgt
-            wq = codes.tile([P, 2, 512], U32, align_bytes=64)
-            ws = codes.tile([P, 2, 512], U8, align_bytes=64)
-            mq = codes.tile([P, 2, 512], U32, align_bytes=64)
-            ms = codes.tile([P, 2, 512], U8, align_bytes=64)
-            cw[i] = (wq, ws, mq, ms)
-            sbt = codes.tile([P, 512], F32)
-            sb[i] = sbt
+        finals = {0: [], 1: [0]}
+        feeds = {(0, 2): 6, (3, 3): 4}
+        state = {}
 
-            late = {"add": 0, "mx": 3}
+        def s_work(u, slot):
+            pending, ahead, k = state["p"], state["a"], state["k"]
+            for n in range(feeds.get((u, slot), 0)):
+                act_a(*pending.pop(0))
+                if len(pending) > ahead - 1:
+                    rho_t(*pending[ahead - 1])
+                if not pending:
+                    for f in finals[k]:
+                        final(f, 0, 4)
+                        final(f, 4, 4)
+                    act_l(GROUPS[k + 1])
 
-            def adds_of_last_chunk(n):
-                for q in range(n):
-                    if i > 0 and late["add"] < NB:
-                        add_s(i - 1, late["add"])
-                        late["add"] = late["add"] + 1
-                        if late["mx"] < NB:
-                            mx_tile(i - 1, late["mx"])
-                            late["mx"] = late["mx"] + 1
+        for k, units in enumerate(GROUPS):
+            nxt = GROUPS[k + 1] if k + 1 < len(GROUPS) else []
+            pending = [(u, b) for u in nxt for b in range(2)]
+            ahead = min(6 if k == 0 else 2, len(pending))
+            state["p"], state["a"], state["k"] = pending, ahead, k
+            for n in range(ahead):
+                rho_t(*pending[n], k == 0 and n < 4)
+            if k > 0:
+                for u in units:
+                    act_d(u)
 
-            nxt = i + 1 < NCH
-            nxt2 = i + 2 < NCH
-            for u in range(4):
-                act_d(i, u)
-            if nxt:
-                chain_n = chain_pool.tile([P, 4, 512, 2], F32, tag="chain")
-                chain[i + 1] = chain_n
-                act_a(i + 1, 0)
-                act_a(i + 1, 1)
-                act_a(i + 1, 2)
-            if nxt2:
-                load_cls(rho_raw, rho, i + 2, ("r", False))
-            adds_of_last_chunk(2)
-            dve_t(i, 0)
-            adds_of_last_chunk(1)
-            dve_t(i, 1)
-            cast(wg[i], chain[i], 0, 0.5)
-            adds_of_last_chunk(1)
-            if nxt:
-                rho_t(i + 1, 3)
-                act_a(i + 1, 3)
-                act_l(i + 1)
-            dve_v(i, 0)
-            if nxt2:
-                rho_t(i + 2, 0)
-            mean_t(i, 2)
-            adds_of_last_chunk(1)
-            dve_v(i, 1)
-            adds_of_last_chunk(NB)
-            if nxt2:
-                rho_t(i + 2, 1)
-            ones_mm(i, 0, 0)
-            mean_t(i, 3)
-            if nxt2:
-                rho_t(i + 2, 2)
-            cast(mwg[i], tprod[i], 0, -1.0)
-            cast(wg[i], chain[i], 1, 0.5)
-            if nxt2:
-                load_cls(mean_raw, mean, i + 2, ("m", False))
-            dve_t(i, 2)
-            dve_v(i, 2)
-            if nxt:
-                mean_t(i + 1, 0)
-            dve_t(i, 3)
-            cast(mwg[i], tprod[i], 1, -1.0)
-            dve_v(i, 3)
-            ones_mm(i, 0, 1)
-            if nxt:
-                mean_t(i + 1, 1)
-            ones_mm(i, 1, 0)
-            ones_mm(i, 1, 1)
-            quant(wg[i], wq, ws, 0)
-            quant(mwg[i], mq, ms, 0)
-            quant(wg[i], wq, ws, 1)
-            evac_s(i, 0)
-            quant(mwg[i], mq, ms, 1)
-            evac_s(i, 1)
-            if nxt:
-                for bt in range(3):
-                    mx_tile(i, bt)
-            else:
-                for b0 in range(0, NB, 2):
-                    final(0, b0, 2)
-                for bt in range(NB):
-                    mx_tile(i, bt)
-                    add_s(i, bt)
+            for u in units:
+                last = u == NU - 1
+                s_work(u, 0)
+                cast_w(u)
+                dve_t(u, 0)
+                cast_mw(u, 0)
+                dve_t(u, 1)
+                cast_mw(u, 1)
+                s_work(u, 1)
+                if u > 0:
+                    evac_s(u - 1)
+                    mx_pair(u - 1, 2)
+                if last:
+                    add_s(u - 1, 0)
+                    mx_pair(u - 1, 3)
+                    quant_w(u)
+                dve_v(u, 0)
+                if not last:
+                    mean_t(u + 1, 0)
+                dve_v(u, 1)
+                if not last:
+                    mean_t(u + 1, 1)
+                add_v(u)
+                s_work(u, 2)
+                if last:
+                    quant_mw(u)
+                    for q in range(1, 4):
+                        add_s(u - 1, q)
+                    break
+                if u > 0:
+                    add_s(u - 1, 0)
+                    mx_pair(u - 1, 3)
+                    add_s(u - 1, 1)
+                if u + 3 < NU:
+                    load_mean(u + 3)
+                if u == 0:
+                    load_rho(6)
+                    load_rho(7)
+                s_work(u, 3)
+                if u > 0:
+                    add_s(u - 1, 2)
+                    add_s(u - 1, 3)
+                ones_mm(u)
+                quant_w(u)
+                quant_mw(u)
+                mx_pair(u, 0)
+                mx_pair(u, 1)
+                s_work(u, 4)
 
-        for i in range(1, NCH - 1):
-            for b0 in range(0, NB, 2):
-                final(i, b0, 2)
-        for b0 in range(NB):
-            final(NCH - 1, b0, 1)
+        for u in range(1, 7):
+            final(u, 0, 4)
+            final(u, 4, 4)
+        u = NU - 1
+        mx_pair(u, 0)
+        mx_pair(u, 1)
+        ones_mm(u)
+        mx_pair(u, 2)
+        evac_s(u)
+        for q in range(4):
+            add_s(u, q)
+            final(u, 2 * q, 2)
+            if q == 0:
+                mx_pair(u, 3)

@@ -9,8 +9,9 @@ P = 128
 NB = 8
 NU = 8
 UC = 256
-X2_G = range(8)
-RS = False
+NR = 2
+NX = 6
+NM = 1
 GROUPS = [[0, 1, 2], [3, 4, 5], [6, 7]]
 F32 = mybir.dt.float32
 BF16 = mybir.dt.bfloat16
@@ -46,8 +47,7 @@ def tile_dynamic_estimator_kernel(tc, x, mean, rho, out):
         tprod = {}
         vprod = {}
         vsum = {}
-        wg = {}
-        mwg = {}
+        pair = {}
         cw = {}
         sb = {}
         pre = {}
@@ -167,16 +167,16 @@ def tile_dynamic_estimator_kernel(tc, x, mean, rho, out):
                 out=part(vprod[u], g), in0=mts[(u, g)][:].bitcast(BF16), in1=part(tprod[u], g), op=ALU.mult
             )
 
-        def add_v(u):
+        def add_v(eng, u):
             vs = work.tile([P, 2, UC, 2], F32)
             vsum[u] = vs
-            nc.gpsimd.tensor_tensor(
+            eng.tensor_tensor(
                 out=flat(vs), in0=part(vprod[u], 0), in1=part(vprod[u], 1), op=ALU.add
             )
 
-        def cast(dst, src, g, factor):
+        def cast(u, w, g, src, factor):
             nc.gpsimd.tensor_scalar(
-                out=dst[:, g, :, :].rearrange("p c (u e) -> p c u e", u=2),
+                out=pair[u][:, w, g, :, :].rearrange("p c (u e) -> p c u e", u=2),
                 in0=src[:, 2 * g : 2 * g + 2, :, :].rearrange("p u c e -> p c u e"),
                 scalar1=factor,
                 scalar2=0.0,
@@ -185,47 +185,31 @@ def tile_dynamic_estimator_kernel(tc, x, mean, rho, out):
             )
 
         def cast_w(u):
-            wgt = work.tile([P, 2, UC, 4], BF16, align_bytes=64)
-            wg[u] = wgt
+            pt = work.tile([P, 2, 2, UC, 4], BF16, align_bytes=64)
+            pair[u] = pt
             for g in range(2):
-                cast(wgt, chain[u], g, 0.5)
+                cast(u, 0, g, chain[u], 0.5)
 
         def cast_mw(u, g):
-            if g == 0:
-                mwgt = work.tile([P, 2, UC, 4], BF16, align_bytes=64)
-                mwg[u] = mwgt
-            cast(mwg[u], tprod[u], g, -1.0)
+            cast(u, 1, g, tprod[u], -1.0)
 
-        def quant(src, q_t, s_t):
+        def quant(u):
+            qt = codes.tile([P, 2, 2, UC], U32, align_bytes=64)
+            st = codes.tile([P, 2, 2, UC], U8, align_bytes=64)
+            cw[u] = (qt, st)
             nc.vector.quantize_mx(
-                out=q_t[:].rearrange("p g c -> p (g c)").bitcast(FP8X4),
-                scales=s_t[:].rearrange("p g c -> p (g c)"),
-                in_=src[:].rearrange("p g c t -> p (g c t)"),
+                out=qt[:].rearrange("p w g c -> p (w g c)").bitcast(FP8X4),
+                scales=st[:].rearrange("p w g c -> p (w g c)"),
+                in_=pair[u][:].rearrange("p w g c t -> p (w g c t)"),
             )
-
-        def quant_w(u):
-            wq = codes.tile([P, 2, UC], U32, align_bytes=64)
-            ws = codes.tile([P, 2, UC], U8, align_bytes=64)
-            cw[(u, 0)] = (wq, ws)
-            quant(wg[u], wq, ws)
-
-        def quant_mw(u):
-            mq = codes.tile([P, 2, UC], U32, align_bytes=64)
-            ms = codes.tile([P, 2, UC], U8, align_bytes=64)
-            cw[(u, 1)] = (mq, ms)
-            quant(mwg[u], mq, ms)
 
         def ones_mm(u):
             ss = ps_acc.tile([P, UC], F32, tag="acc")
             ssum[u] = ss
             for n in range(4):
-                uu, e = divmod(n, 2)
+                j, e = divmod(n, 2)
                 nc.tensor.matmul(
-                    out=ss[:],
-                    lhsT=half[:],
-                    rhs=vsum[u][:, uu, :, e],
-                    start=(n == 0),
-                    stop=(n == 3),
+                    out=ss[:], lhsT=half[:], rhs=vsum[u][:, j, :, e], start=(n == 0), stop=(n == 3)
                 )
 
         def evac_s(u):
@@ -236,21 +220,20 @@ def tile_dynamic_estimator_kernel(tc, x, mean, rho, out):
         def mx_pair(u, q):
             acc = ps_acc.tile([P, 2, UC], F32, tag="acc")
             accs[(u, q)] = acc
-            wq, ws = cw[(u, 0)]
-            mq, ms = cw[(u, 1)]
+            qt, st = cw[u]
             for r in range(2):
                 bt = 2 * q + r
                 ops = []
                 for g in range(2):
-                    ops.append((x2q, x2s, wq, ws, g))
-                    ops.append((xq, xs, mq, ms, g))
-                for n, (lq, ls, rq, rs, g) in enumerate(ops):
+                    ops.append((x2q, x2s, 0, g))
+                    ops.append((xq, xs, 1, g))
+                for n, (lq, ls, w, g) in enumerate(ops):
                     nc.tensor.matmul_mx(
                         out=acc[:, r, :],
                         lhsT=lq[:, bt, g * 128 : (g + 1) * 128].bitcast(FP8X4),
                         lhsT_scale=ls[:, bt, g * 128 : (g + 1) * 128],
-                        rhs=rq[:, g, :].bitcast(FP8X4),
-                        rhs_scale=rs[:, g, :],
+                        rhs=qt[:, w, g, :].bitcast(FP8X4),
+                        rhs_scale=st[:, w, g, :],
                         start=(n == 0),
                         stop=(n == 3),
                     )
@@ -277,6 +260,7 @@ def tile_dynamic_estimator_kernel(tc, x, mean, rho, out):
             )
 
         xgs = {}
+        x2gs = {}
 
         def x_turn(bt):
             px = ps_mean.tile([P, 4, 128], F32, tag="mean")
@@ -287,23 +271,27 @@ def tile_dynamic_estimator_kernel(tc, x, mean, rho, out):
             nc.vector.tensor_copy(
                 out=xg[:].bitcast(F32), in_=px[:].rearrange("p (g u) b -> p g b u", g=2)
             )
+            xgs[bt] = xg
+
+        def x_square(bt):
             x2g = xstage.tile([P, 2, 128, 4], BF16, align_bytes=64)
-            eng = nc.gpsimd if bt in X2_G else nc.vector
-            eng.tensor_tensor(out=x2g[:], in0=xg[:], in1=xg[:], op=ALU.mult)
-            xgs[bt] = (xg, x2g)
+            nc.vector.tensor_tensor(out=x2g[:], in0=xgs[bt][:], in1=xgs[bt][:], op=ALU.mult)
+            x2gs[bt] = x2g
 
         def x_quant(bt, w):
             q_t, s_t = ((xq, xs), (x2q, x2s))[w]
             nc.vector.quantize_mx(
                 out=q_t[:, bt, :].bitcast(FP8X4), scales=s_t[:, bt, :],
-                in_=xgs[bt][w][:].rearrange("p g b t -> p (g b t)"),
+                in_=(xgs, x2gs)[w][bt][:].rearrange("p g b t -> p (g b t)"),
             )
 
         def act_l1(u):
             nc.scalar.activation(out=flat(chain[u]), in_=flat(chain[u]), func=ACT.Ln, bias=one_col[:])
 
-        def square(eng, u):
-            eng.tensor_tensor(out=flat(chain[u]), in0=flat(chain[u]), in1=flat(chain[u]), op=ALU.mult)
+        def square(u, g):
+            nc.vector.tensor_tensor(
+                out=part(chain[u], g), in0=part(chain[u], g), in1=part(chain[u], g), op=ALU.mult
+            )
 
         def act_r(u):
             for g in range(2):
@@ -311,44 +299,51 @@ def tile_dynamic_estimator_kernel(tc, x, mean, rho, out):
                     out=part(chain[u], g), in_=part(chain[u], g), func=ACT.Abs_reciprocal_sqrt
                 )
 
+        def x_step(n):
+            if n < NB:
+                x_turn(n)
+            if 0 <= n - 1 < NB:
+                x_square(n - 1)
+                x_quant(n - 1, 0)
+            if 0 <= n - 2 < NB:
+                x_quant(n - 2, 1)
+
         banks = [(u, b) for u in GROUPS[0] for b in range(2)]
         rho_t(*banks[0])
         rho_t(*banks[1])
-        for n in range(NB):
+        xb = 0
+        for n in range(max(len(banks), NX)):
             if n < len(banks):
                 act_a(*banks[n])
-            x_turn(n)
+            if n < NX:
+                x_step(n)
+                xb = n + 1
             if n + 2 < len(banks):
                 rho_t(*banks[n + 2])
-            if n > 0:
-                x_quant(n - 1, 0)
-                x_quant(n - 1, 1)
         for u in GROUPS[0]:
             act_l1(u)
         load_rho(5)
-        if RS:
-            square(nc.vector, 0)
-            square(nc.gpsimd, 1)
-            square(nc.vector, 0)
-            x_quant(7, 0)
-            x_quant(7, 1)
-            square(nc.vector, 1)
-            square(nc.vector, 2)
-            square(nc.vector, 2)
-            for u in GROUPS[0]:
-                act_r(u)
-        else:
-            for u in GROUPS[0]:
-                nc.scalar.activation(out=flat(chain[u]), in_=flat(chain[u]), func=ACT.Ln)
-            x_quant(7, 0)
-            x_quant(7, 1)
-            for u in GROUPS[0]:
-                act_d(u)
+        for u in GROUPS[0][NR:]:
+            nc.scalar.activation(out=flat(chain[u]), in_=flat(chain[u]), func=ACT.Ln)
+        for u in GROUPS[0][:NR]:
+            for n in range(2):
+                for g in range(2):
+                    square(u, g)
+            act_r(u)
+            for n in range(NM):
+                if xb < NB + 2:
+                    x_step(xb)
+                    xb = xb + 1
+        for u in GROUPS[0][NR:]:
+            act_d(u)
+        while xb < NB + 2:
+            x_step(xb)
+            xb = xb + 1
         mean_t(0, 0)
         mean_t(0, 1)
 
         finals = {0: [], 1: [0]}
-        feeds = {(0, 2): 6, (3, 3): 4}
+        feeds = {(0, 2): 6, (3, 1): 4}
         state = {}
 
         def s_work(u, slot):
@@ -376,64 +371,51 @@ def tile_dynamic_estimator_kernel(tc, x, mean, rho, out):
 
             for u in units:
                 last = u == NU - 1
-                s_work(u, 0)
                 cast_w(u)
                 dve_t(u, 0)
                 cast_mw(u, 0)
                 dve_t(u, 1)
                 cast_mw(u, 1)
-                s_work(u, 1)
+                dve_v(u, 0)
                 if u > 0:
                     evac_s(u - 1)
-                    mx_pair(u - 1, 2)
-                if last:
-                    add_s(u - 1, 0)
                     mx_pair(u - 1, 3)
-                    quant_w(u)
-                dve_v(u, 0)
-                if not last:
-                    mean_t(u + 1, 0)
                 dve_v(u, 1)
-                if not last:
-                    mean_t(u + 1, 1)
-                add_v(u)
-                s_work(u, 2)
+                s_work(u, 1)
                 if last:
-                    quant_mw(u)
-                    for q in range(1, 4):
-                        add_s(u - 1, q)
-                    break
-                if u > 0:
-                    add_s(u - 1, 0)
-                    mx_pair(u - 1, 3)
-                    add_s(u - 1, 1)
+                    add_v(nc.vector, u)
+                    ones_mm(u)
+                else:
+                    mean_t(u + 1, 0)
+                    mean_t(u + 1, 1)
+                    add_v(nc.gpsimd, u)
                 if u + 3 < NU:
                     load_mean(u + 3)
                 if u == 0:
                     load_rho(6)
                     load_rho(7)
-                s_work(u, 3)
+                s_work(u, 2)
                 if u > 0:
+                    add_s(u - 1, 0)
+                    add_s(u - 1, 1)
+                    if last:
+                        quant(u)
                     add_s(u - 1, 2)
                     add_s(u - 1, 3)
-                ones_mm(u)
-                quant_w(u)
-                quant_mw(u)
-                mx_pair(u, 0)
-                mx_pair(u, 1)
-                s_work(u, 4)
+                if last:
+                    evac_s(u)
+                else:
+                    quant(u)
+                    ones_mm(u)
+                for q in range(3):
+                    mx_pair(u, q)
+                s_work(u, 3)
 
         for u in range(1, 7):
             final(u, 0, 4)
             final(u, 4, 4)
         u = NU - 1
-        mx_pair(u, 0)
-        mx_pair(u, 1)
-        ones_mm(u)
-        mx_pair(u, 2)
-        evac_s(u)
+        mx_pair(u, 3)
         for q in range(4):
             add_s(u, q)
             final(u, 2 * q, 2)
-            if q == 0:
-                mx_pair(u, 3)

from contextlib import ExitStack

import concourse.mybir as mybir
from concourse.masks import make_identity

FLOPS = 2 * 2 * 1024 * 2048 * 1024

P = 128
NB = 8
NU = 8
UC = 256
NR = 2
NX = 6
NM = 1
GROUPS = [[0, 1, 2], [3, 4, 5], [6, 7]]
F32 = mybir.dt.float32
BF16 = mybir.dt.bfloat16
U32 = mybir.dt.uint32
U8 = mybir.dt.uint8
FP8X4 = mybir.dt.float8_e4m3fn_x4
ACT = mybir.ActivationFunctionType
ALU = mybir.AluOpType


def tile_dynamic_estimator_kernel(tc, x, mean, rho, out):
    nc = tc.nc
    with ExitStack() as ctx:
        consts = ctx.enter_context(tc.tile_pool(name="consts", bufs=1))
        xraw_pool = ctx.enter_context(tc.tile_pool(name="xraw", bufs=2))
        xstage = ctx.enter_context(tc.tile_pool(name="xstage", bufs=4))
        xkeep = ctx.enter_context(tc.tile_pool(name="xkeep", bufs=1))
        rho_pool = ctx.enter_context(tc.tile_pool(name="rho", bufs=5))
        mean_pool = ctx.enter_context(tc.tile_pool(name="mean", bufs=3))
        chain_pool = ctx.enter_context(tc.tile_pool(name="chain", bufs=6))
        work = ctx.enter_context(tc.tile_pool(name="work", bufs=2))
        codes = ctx.enter_context(tc.tile_pool(name="codes", bufs=2))
        pre_pool = ctx.enter_context(tc.tile_pool(name="pre", bufs=5))
        ps_rho = ctx.enter_context(tc.psum_pool(name="ps_rho", bufs=2))
        ps_mean = ctx.enter_context(tc.psum_pool(name="ps_mean", bufs=2))
        ps_acc = ctx.enter_context(tc.psum_pool(name="ps_acc", bufs=4))
        ctx.enter_context(tc.manual_schedule())

        rho_raw = {}
        mean_raw = {}
        x_raw = {}
        chain = {}
        tprod = {}
        vprod = {}
        vsum = {}
        pair = {}
        cw = {}
        sb = {}
        pre = {}
        rts = {}
        mts = {}
        ssum = {}
        accs = {}

        def load_rho(u):
            rr = rho_pool.tile([P, 2, 1024], BF16)
            nc.sync.dma_start(
                out=rr[:], in_=rho[u * UC : (u + 1) * UC, :].rearrange("(b p) k -> p b k", p=P)
            )
            rho_raw[u] = rr

        def load_mean(u):
            mr = mean_pool.tile([P, 2, 1024], BF16)
            nc.sync.dma_start(
                out=mr[:], in_=mean[u * UC : (u + 1) * UC, :].rearrange("(b p) k -> p b k", p=P)
            )
            mean_raw[u] = mr

        def load_x(q):
            xr = xraw_pool.tile([P, 2, 1024], BF16)
            nc.sync.dma_start(
                out=xr[:], in_=x[q * 256 : (q + 1) * 256, :].rearrange("(b p) k -> p b k", p=P)
            )
            x_raw[q] = xr

        load_rho(0)
        load_x(0)
        load_rho(1)
        load_x(1)
        load_rho(2)
        for q in range(2, 4):
            load_x(q)
        load_mean(0)
        load_rho(3)
        load_mean(1)
        load_rho(4)
        load_mean(2)

        ident = consts.tile([P, P], F32)
        make_identity(nc, ident[:])
        half = consts.tile([P, P], F32)
        nc.vector.memset(half[:], 0.5)
        one_col = consts.tile([P, 1], F32)
        nc.vector.memset(one_col[:], 1.0)

        xq = xkeep.tile([P, NB, 256], U32, align_bytes=64)
        xs = xkeep.tile([P, NB, 256], U8, align_bytes=64)
        x2q = xkeep.tile([P, NB, 256], U32, align_bytes=64)
        x2s = xkeep.tile([P, NB, 256], U8, align_bytes=64)

        def part(t, g):
            return t[:, 2 * g : 2 * g + 2, :, :].rearrange("p u c e -> p u (c e)")

        def rho_t(u, b, spare=False):
            if spare:
                pt = ps_acc.tile([P, 4, 128], F32, tag="acc")
            else:
                pt = ps_rho.tile([P, 4, 128], F32, tag="rho")
            words = rho_raw[u][:, b, :].bitcast(F32)
            for j in range(4):
                nc.tensor.transpose(pt[:, j, :], words[:, j * 128 : (j + 1) * 128], ident[:])
            rts[(u, b)] = pt

        def act_a(u, b):
            if b == 0:
                ch = chain_pool.tile([P, 4, UC, 2], F32)
                chain[u] = ch
            nc.scalar.activation(
                out=chain[u][:, :, b * 128 : (b + 1) * 128, :].rearrange("p j c e -> p j (c e)"),
                in_=rts[(u, b)][:].bitcast(BF16),
                func=ACT.Exp,
            )

        def flat(t):
            return t[:].rearrange("p u c e -> p (u c e)")

        def act_l(units):
            for u in units:
                nc.scalar.activation(out=flat(chain[u]), in_=flat(chain[u]), func=ACT.Ln, bias=one_col[:])
            for u in units:
                nc.scalar.activation(out=flat(chain[u]), in_=flat(chain[u]), func=ACT.Ln)

        def act_d(u):
            for g in range(2):
                nc.scalar.activation(
                    out=part(chain[u], g), in_=part(chain[u], g), func=ACT.Exp, scale=-2.0
                )

        def mean_t(u, g):
            pm = ps_mean.tile([P, 2, 256], F32, tag="mean")
            for uu in range(2):
                for cb in range(2):
                    words = mean_raw[u][:, cb, :].bitcast(F32)
                    j = 2 * g + uu
                    nc.tensor.transpose(
                        pm[:, uu, cb * 128 : (cb + 1) * 128], words[:, j * 128 : (j + 1) * 128], ident[:]
                    )
            mts[(u, g)] = pm

        def dve_t(u, g):
            if g == 0:
                tp = work.tile([P, 4, UC, 2], F32)
                tprod[u] = tp
            nc.vector.tensor_tensor(
                out=part(tprod[u], g), in0=mts[(u, g)][:].bitcast(BF16), in1=part(chain[u], g), op=ALU.mult
            )

        def dve_v(u, g):
            if g == 0:
                vp = work.tile([P, 4, UC, 2], F32)
                vprod[u] = vp
            nc.vector.tensor_tensor(
                out=part(vprod[u], g), in0=mts[(u, g)][:].bitcast(BF16), in1=part(tprod[u], g), op=ALU.mult
            )

        def add_v(eng, u):
            vs = work.tile([P, 2, UC, 2], F32)
            vsum[u] = vs
            eng.tensor_tensor(
                out=flat(vs), in0=part(vprod[u], 0), in1=part(vprod[u], 1), op=ALU.add
            )

        def cast(u, w, g, src, factor):
            nc.gpsimd.tensor_scalar(
                out=pair[u][:, w, g, :, :].rearrange("p c (u e) -> p c u e", u=2),
                in0=src[:, 2 * g : 2 * g + 2, :, :].rearrange("p u c e -> p c u e"),
                scalar1=factor,
                scalar2=0.0,
                op0=ALU.mult,
                op1=ALU.add,
            )

        def cast_w(u):
            pt = work.tile([P, 2, 2, UC, 4], BF16, align_bytes=64)
            pair[u] = pt
            for g in range(2):
                cast(u, 0, g, chain[u], 0.5)

        def cast_mw(u, g):
            cast(u, 1, g, tprod[u], -1.0)

        def quant(u):
            qt = codes.tile([P, 2, 2, UC], U32, align_bytes=64)
            st = codes.tile([P, 2, 2, UC], U8, align_bytes=64)
            cw[u] = (qt, st)
            nc.vector.quantize_mx(
                out=qt[:].rearrange("p w g c -> p (w g c)").bitcast(FP8X4),
                scales=st[:].rearrange("p w g c -> p (w g c)"),
                in_=pair[u][:].rearrange("p w g c t -> p (w g c t)"),
            )

        def ones_mm(u):
            ss = ps_acc.tile([P, UC], F32, tag="acc")
            ssum[u] = ss
            for n in range(4):
                j, e = divmod(n, 2)
                nc.tensor.matmul(
                    out=ss[:], lhsT=half[:], rhs=vsum[u][:, j, :, e], start=(n == 0), stop=(n == 3)
                )

        def evac_s(u):
            sbt = codes.tile([P, UC], F32)
            sb[u] = sbt
            nc.vector.tensor_copy(out=sbt[:], in_=ssum[u][:])

        def mx_pair(u, q):
            acc = ps_acc.tile([P, 2, UC], F32, tag="acc")
            accs[(u, q)] = acc
            qt, st = cw[u]
            for r in range(2):
                bt = 2 * q + r
                ops = []
                for g in range(2):
                    ops.append((x2q, x2s, 0, g))
                    ops.append((xq, xs, 1, g))
                for n, (lq, ls, w, g) in enumerate(ops):
                    nc.tensor.matmul_mx(
                        out=acc[:, r, :],
                        lhsT=lq[:, bt, g * 128 : (g + 1) * 128].bitcast(FP8X4),
                        lhsT_scale=ls[:, bt, g * 128 : (g + 1) * 128],
                        rhs=qt[:, w, g, :].bitcast(FP8X4),
                        rhs_scale=st[:, w, g, :],
                        start=(n == 0),
                        stop=(n == 3),
                    )

        def add_s(u, q):
            if q == 0:
                pre_t = pre_pool.tile([P, NB, UC], F32)
                pre[u] = pre_t
            nc.vector.tensor_tensor(
                out=pre[u][:, 2 * q : 2 * q + 2, :],
                in0=accs[(u, q)][:],
                in1=sb[u][:].unsqueeze(1).to_broadcast([P, 2, UC]),
                op=ALU.add,
            )

        def final(u, b0, nb):
            sl = pre[u][:, b0 : b0 + nb, :]
            nc.scalar.activation(out=sl, in_=sl, func=ACT.Exp, scale=-1.0)
            nc.sync.dma_start(
                out=out[b0 * P : (b0 + nb) * P, u * UC : (u + 1) * UC].rearrange(
                    "(t p) c -> p t c", p=P
                ),
                in_=sl,
            )

        xgs = {}
        x2gs = {}

        def x_turn(bt):
            px = ps_mean.tile([P, 4, 128], F32, tag="mean")
            words = x_raw[bt // 2][:, bt % 2, :].bitcast(F32)
            for j in range(4):
                nc.tensor.transpose(px[:, j, :], words[:, j * 128 : (j + 1) * 128], ident[:])
            xg = xstage.tile([P, 2, 128, 4], BF16, align_bytes=64)
            nc.vector.tensor_copy(
                out=xg[:].bitcast(F32), in_=px[:].rearrange("p (g u) b -> p g b u", g=2)
            )
            xgs[bt] = xg

        def x_square(bt):
            x2g = xstage.tile([P, 2, 128, 4], BF16, align_bytes=64)
            nc.vector.tensor_tensor(out=x2g[:], in0=xgs[bt][:], in1=xgs[bt][:], op=ALU.mult)
            x2gs[bt] = x2g

        def x_quant(bt, w):
            q_t, s_t = ((xq, xs), (x2q, x2s))[w]
            nc.vector.quantize_mx(
                out=q_t[:, bt, :].bitcast(FP8X4), scales=s_t[:, bt, :],
                in_=(xgs, x2gs)[w][bt][:].rearrange("p g b t -> p (g b t)"),
            )

        def act_l1(u):
            nc.scalar.activation(out=flat(chain[u]), in_=flat(chain[u]), func=ACT.Ln, bias=one_col[:])

        def square(u, g):
            nc.vector.tensor_tensor(
                out=part(chain[u], g), in0=part(chain[u], g), in1=part(chain[u], g), op=ALU.mult
            )

        def act_r(u):
            for g in range(2):
                nc.scalar.activation(
                    out=part(chain[u], g), in_=part(chain[u], g), func=ACT.Abs_reciprocal_sqrt
                )

        def x_step(n):
            if n < NB:
                x_turn(n)
            if 0 <= n - 1 < NB:
                x_square(n - 1)
                x_quant(n - 1, 0)
            if 0 <= n - 2 < NB:
                x_quant(n - 2, 1)

        banks = [(u, b) for u in GROUPS[0] for b in range(2)]
        rho_t(*banks[0])
        rho_t(*banks[1])
        xb = 0
        for n in range(max(len(banks), NX)):
            if n < len(banks):
                act_a(*banks[n])
            if n < NX:
                x_step(n)
                xb = n + 1
            if n + 2 < len(banks):
                rho_t(*banks[n + 2])
        for u in GROUPS[0]:
            act_l1(u)
        load_rho(5)
        for u in GROUPS[0][NR:]:
            nc.scalar.activation(out=flat(chain[u]), in_=flat(chain[u]), func=ACT.Ln)
        for u in GROUPS[0][:NR]:
            for n in range(2):
                for g in range(2):
                    square(u, g)
            act_r(u)
            for n in range(NM):
                if xb < NB + 2:
                    x_step(xb)
                    xb = xb + 1
        for u in GROUPS[0][NR:]:
            act_d(u)
        while xb < NB + 2:
            x_step(xb)
            xb = xb + 1
        mean_t(0, 0)
        mean_t(0, 1)

        finals = {0: [], 1: [0]}
        feeds = {(0, 2): 6, (3, 1): 4}
        state = {}

        def s_work(u, slot):
            pending, ahead, k = state["p"], state["a"], state["k"]
            for n in range(feeds.get((u, slot), 0)):
                act_a(*pending.pop(0))
                if len(pending) > ahead - 1:
                    rho_t(*pending[ahead - 1])
                if not pending:
                    for f in finals[k]:
                        final(f, 0, 4)
                        final(f, 4, 4)
                    act_l(GROUPS[k + 1])

        for k, units in enumerate(GROUPS):
            nxt = GROUPS[k + 1] if k + 1 < len(GROUPS) else []
            pending = [(u, b) for u in nxt for b in range(2)]
            ahead = min(6 if k == 0 else 2, len(pending))
            state["p"], state["a"], state["k"] = pending, ahead, k
            for n in range(ahead):
                rho_t(*pending[n], k == 0 and n < 4)
            if k > 0:
                for u in units:
                    act_d(u)

            for u in units:
                last = u == NU - 1
                cast_w(u)
                dve_t(u, 0)
                cast_mw(u, 0)
                dve_t(u, 1)
                cast_mw(u, 1)
                dve_v(u, 0)
                if u > 0:
                    evac_s(u - 1)
                    mx_pair(u - 1, 3)
                dve_v(u, 1)
                s_work(u, 1)
                if last:
                    add_v(nc.vector, u)
                    ones_mm(u)
                else:
                    mean_t(u + 1, 0)
                    mean_t(u + 1, 1)
                    add_v(nc.gpsimd, u)
                if u + 3 < NU:
                    load_mean(u + 3)
                if u == 0:
                    load_rho(6)
                    load_rho(7)
                s_work(u, 2)
                if u > 0:
                    add_s(u - 1, 0)
                    add_s(u - 1, 1)
                    if last:
                        quant(u)
                    add_s(u - 1, 2)
                    add_s(u - 1, 3)
                if last:
                    evac_s(u)
                else:
                    quant(u)
                    ones_mm(u)
                for q in range(3):
                    mx_pair(u, q)
                s_work(u, 3)

        for u in range(1, 7):
            final(u, 0, 4)
            final(u, 4, 4)
        u = NU - 1
        mx_pair(u, 3)
        for q in range(4):
            add_s(u, q)
            final(u, 2 * q, 2)
